import numpy as np
import ml_dtypes

BF16 = ml_dtypes.bfloat16


def bf(x):
    return np.asarray(x, np.float32).astype(BF16)


def f32(x):
    return np.asarray(x, np.float32)


def f64(x):
    return np.asarray(x).astype(np.float64)


def striped(idx):
    return np.tile(idx.reshape(-1, 16).T, (8, 1))


D, V, B, T, N = 512, 4096, 4, 512, 2048


def positional(seq_len, dim):
    position = np.arange(seq_len, dtype=np.float32)[:, None]
    div_term = np.exp(np.arange(0, dim, 2, dtype=np.float32) * np.float32(-(np.log(10000.0) / dim)))
    ang = position * div_term
    pe = np.zeros((seq_len, dim), np.float32)
    pe[:, 0::2] = np.sin(ang)
    pe[:, 1::2] = np.cos(ang)
    return np.ascontiguousarray(pe.T)


def setup_inputs():
    return {
        "table": f32(np.random.standard_normal((D, V))),
        "pe": f32(positional(T, D)),
        "wq": bf(np.random.standard_normal((D, D)) / np.sqrt(D)),
        "bq": f32(0.2 * np.random.standard_normal((D, 1))),
        "wk": bf(np.random.standard_normal((D, D)) / np.sqrt(D)),
        "wv": bf(np.random.standard_normal((D, D)) / np.sqrt(D)),
        "bv": f32(0.1 * np.random.standard_normal((D, 1))),
        "offs": striped(np.random.permutation(np.tile(np.arange(V), 2))[:N]),
    }


def reference(table, pe, wq, bq, wk, wv, bv, offs):
    idx = offs[:16].T.reshape(-1)
    e = f64(table)[:, idx] + np.tile(f64(pe), (1, B))
    q = f64(wq).T @ e + f64(bq)
    k = f64(wk).T @ e
    v = f64(wv).T @ e + f64(bv)
    res = np.zeros((D, N), np.float64)
    for b in range(B):
        sl = slice(b * T, (b + 1) * T)
        s = q[:, sl].T @ k[:, sl] / np.sqrt(D)
        s = s - s.max(axis=1, keepdims=True)
        p = np.exp(s)
        a = p / p.sum(axis=1, keepdims=True)
        res[:, sl] = v[:, sl] @ a.T
    return res

@@ -1,0 +1,157 @@
+import math
+from contextlib import ExitStack
+
+import concourse.mybir as mybir
+from concourse.masks import make_identity
+
+P = 128
+D = 512
+V = 4096
+B = 4
+T = 512
+NB = D // P
+assert T // P == NB
+
+F32 = mybir.dt.float32
+BF16 = mybir.dt.bfloat16
+U16 = mybir.dt.uint16
+ADD = mybir.AluOpType.add
+FUNC = mybir.ActivationFunctionType
+SCALE = 1.0 / math.sqrt(D)
+
+FLOPS = 3 * 2 * D * D * B * T + 2 * 2 * B * T * T * D
+
+
+def block(i):
+    return slice(i * P, (i + 1) * P)
+
+
+def tile_attentionwithpositionalencoding_b_kernel(tc, table, pe, wq, bq, wk, wv, bv, offs, out):
+    nc = tc.nc
+    with ExitStack() as ctx:
+        held = ctx.enter_context(tc.tile_pool(name="held", bufs=1))
+        pair = ctx.enter_context(tc.tile_pool(name="pair", bufs=2))
+        ring = ctx.enter_context(tc.tile_pool(name="ring", bufs=4))
+        many = ctx.enter_context(tc.tile_pool(name="many", bufs=8))
+        psum = ctx.enter_context(tc.psum_pool(name="psum", bufs=8))
+
+        offsets = held.tile([P, B * T // 16], U16, name="offsets")
+        nc.sync.dma_start(offsets[:], offs)
+        table_sb = [held.tile([P, V], F32, name=f"table{d}") for d in range(NB)]
+        pe_sb = [held.tile([P, T], F32, name=f"pe{d}") for d in range(NB)]
+        wq_sb = [held.tile([P, D], BF16, name=f"wq{d}") for d in range(NB)]
+        wk_sb = [held.tile([P, D], BF16, name=f"wk{d}") for d in range(NB)]
+        wv_sb = [held.tile([P, D], BF16, name=f"wv{d}") for d in range(NB)]
+        for d in range(NB):
+            nc.sync.dma_start(pe_sb[d][:], pe[block(d), :])
+            nc.sync.dma_start(table_sb[d][:], table[block(d), :])
+            nc.sync.dma_start(wq_sb[d][:], wq[block(d), :])
+            nc.sync.dma_start(wk_sb[d][:], wk[block(d), :])
+        for d in range(NB):
+            nc.sync.dma_start(wv_sb[d][:], wv[block(d), :])
+        bv_all = held.tile([P, D], F32, name="bv_all")
+        nc.sync.dma_start(bv_all[:], bv.rearrange("d o -> (d o)").partition_broadcast(P))
+        bq_sb = held.tile([P, NB], F32, name="bq_sb")
+        with nc.allow_non_contiguous_dma(reason="512 biases, one to a partition"):
+            nc.scalar.dma_start(bq_sb[:], bq.rearrange("(m p) o -> p (m o)", p=P))
+        ident = held.tile([P, P], BF16, name="ident")
+        make_identity(nc, ident[:])
+
+        e_bf = [[held.tile([P, T], BF16, name=f"e{d}_{s}") for s in range(B)] for d in range(NB)]
+        for d in range(NB):
+            for s in range(B):
+                e32 = ring.tile([P, T], F32, name="e32")
+                picked = table_sb[d][:].indirect(offsets[:, s * (T // 16) : (s + 1) * (T // 16)])
+                nc.vector.tensor_tensor(e32[:], picked, pe_sb[d][:], ADD)
+                nc.scalar.copy(e_bf[d][s][:], e32[:])
+
+        def project_qk(s, by_table_block):
+            q_bf = [pair.tile([P, T], BF16, name=f"q{m}") for m in range(NB)]
+            k_bf = [pair.tile([P, T], BF16, name=f"k{m}") for m in range(NB)]
+
+            def new_sums(m):
+                q_acc = psum.tile([P, T], F32, name=f"q_acc{m}", tag="bank")
+                k_acc = psum.tile([P, T], F32, name=f"k_acc{m}", tag="bank")
+                return q_acc, k_acc
+
+            def add_block(sums, m, d):
+                q_acc, k_acc = sums
+                first, last = d == 0, d == NB - 1
+                nc.tensor.matmul(q_acc[:], wq_sb[d][:, block(m)], e_bf[d][s][:], start=first, stop=last)
+                nc.tensor.matmul(k_acc[:], wk_sb[d][:, block(m)], e_bf[d][s][:], start=first, stop=last)
+
+            def store(sums, m):
+                q_acc, k_acc = sums
+                nc.scalar.activation(q_bf[m][:], q_acc[:], FUNC.Identity, bias=bq_sb[:, m : m + 1])
+                nc.vector.tensor_copy(k_bf[m][:], k_acc[:])
+
+            if by_table_block:
+                all_sums = [new_sums(m) for m in range(NB)]
+                for d in range(NB):
+                    for m in range(NB):
+                        add_block(all_sums[m], m, d)
+                for m in range(NB):
+                    store(all_sums[m], m)
+            else:
+                for m in range(NB):
+                    sums = new_sums(m)
+                    for d in range(NB):
+                        add_block(sums, m, d)
+                    store(sums, m)
+            return q_bf, k_bf
+
+        def project_v(s):
+            vt_bf = [pair.tile([P, D], BF16, name=f"vt{j}") for j in range(NB)]
+            for j in range(NB):
+                acc = psum.tile([P, D], F32, name="acc", tag="bank")
+                for d in range(NB):
+                    nc.tensor.matmul(acc[:], e_bf[d][s][:, block(j)], wv_sb[d][:], start=(d == 0), stop=(d == NB - 1))
+                nc.vector.tensor_tensor(vt_bf[j][:], acc[:], bv_all[:], ADD)
+            return vt_bf
+
+        def attention_weights(q_bf, k_bf):
+            a_bf = []
+            for i in range(NB):
+                score = psum.tile([P, T], F32, name="score", tag="bank")
+                for m in range(NB):
+                    nc.tensor.matmul(score[:], q_bf[m][:, block(i)], k_bf[m][:], start=(m == 0), stop=(m == NB - 1))
+                top = many.tile([P, 1], F32, name="top")
+                nc.vector.reduce_max(top[:], score[:], axis=mybir.AxisListType.X)
+                shift = many.tile([P, 1], F32, name="shift")
+                nc.vector.tensor_scalar_mul(shift[:], top[:], -SCALE)
+                grown = ring.tile([P, T], F32, name="grown")
+                total = many.tile([P, 1], F32, name="total")
+                nc.scalar.activation(grown[:], score[:], FUNC.Exp, bias=shift[:], scale=SCALE, accum_out=total[:])
+                share = many.tile([P, 1], F32, name="share")
+                nc.vector.reciprocal(share[:], total[:])
+                a_i = many.tile([P, T], BF16, name="a_i")
+                nc.vector.tensor_scalar_mul(a_i[:], grown[:], share[:])
+                a_bf.append(a_i)
+            return a_bf
+
+        def flip(a_bf):
+            at_bf = pair.tile([P, NB, T], BF16, name="at_bf")
+            for i in range(NB):
+                flipped = psum.tile([P, NB, P], BF16, name="flipped", tag="bank")
+                for j in range(NB):
+                    nc.tensor.transpose(flipped[:, j, :], a_bf[i][:, block(j)], ident[:])
+                nc.vector.tensor_copy(at_bf[:, :, block(i)], flipped[:])
+            return at_bf
+
+        def attend(s, vt_bf, at_bf):
+            for m in range(NB):
+                mixed = psum.tile([P, T], F32, name="mixed", tag="bank")
+                for j in range(NB):
+                    nc.tensor.matmul(mixed[:], vt_bf[j][:, block(m)], at_bf[:, j, :], start=(j == 0), stop=(j == NB - 1))
+                out_sb = ring.tile([P, T], F32, name="out_sb")
+                nc.scalar.copy(out_sb[:], mixed[:])
+                nc.sync.dma_start(out[block(m), s * T : (s + 1) * T], out_sb[:])
+
+        q_bf, k_bf = project_qk(0, by_table_block=True)
+        for s in range(B):
+            a_bf = attention_weights(q_bf, k_bf)
+            vt_bf = project_v(s)
+            if s + 1 < B:
+                q_bf, k_bf = project_qk(s + 1, by_table_block=False)
+            at_bf = flip(a_bf)
+            attend(s, vt_bf, at_bf)

@@ -11,6 +11,8 @@ B = 4
 T = 512
 NB = D // P
 assert T // P == NB
+EARLY = (0, 1)
+LATE = (2, 3)
 
 F32 = mybir.dt.float32
 BF16 = mybir.dt.bfloat16
@@ -58,46 +60,39 @@ def tile_attentionwithpositionalencoding_b_kernel(tc, table, pe, wq, bq, wk, wv,
         make_identity(nc, ident[:])
 
         e_bf = [[held.tile([P, T], BF16, name=f"e{d}_{s}") for s in range(B)] for d in range(NB)]
-        for d in range(NB):
+
+        def embed(d):
             for s in range(B):
-                e32 = ring.tile([P, T], F32, name="e32")
+                e32 = pair.tile([P, T], F32, name="e32")
                 picked = table_sb[d][:].indirect(offsets[:, s * (T // 16) : (s + 1) * (T // 16)])
                 nc.vector.tensor_tensor(e32[:], picked, pe_sb[d][:], ADD)
-                nc.scalar.copy(e_bf[d][s][:], e32[:])
+                nc.vector.tensor_copy(e_bf[d][s][:], e32[:])
 
-        def project_qk(s, by_table_block):
-            q_bf = [pair.tile([P, T], BF16, name=f"q{m}") for m in range(NB)]
-            k_bf = [pair.tile([P, T], BF16, name=f"k{m}") for m in range(NB)]
-
-            def new_sums(m):
-                q_acc = psum.tile([P, T], F32, name=f"q_acc{m}", tag="bank")
-                k_acc = psum.tile([P, T], F32, name=f"k_acc{m}", tag="bank")
-                return q_acc, k_acc
-
-            def add_block(sums, m, d):
-                q_acc, k_acc = sums
-                first, last = d == 0, d == NB - 1
+        def sum_qk(s, m, blocks):
+            q_acc = psum.tile([P, T], F32, name="q_acc", tag="bank")
+            k_acc = psum.tile([P, T], F32, name="k_acc", tag="bank")
+            for d in blocks:
+                first, last = d == blocks[0], d == blocks[-1]
                 nc.tensor.matmul(q_acc[:], wq_sb[d][:, block(m)], e_bf[d][s][:], start=first, stop=last)
                 nc.tensor.matmul(k_acc[:], wk_sb[d][:, block(m)], e_bf[d][s][:], start=first, stop=last)
+            return q_acc, k_acc
 
-            def store(sums, m):
-                q_acc, k_acc = sums
-                nc.scalar.activation(q_bf[m][:], q_acc[:], FUNC.Identity, bias=bq_sb[:, m : m + 1])
-                nc.vector.tensor_copy(k_bf[m][:], k_acc[:])
+        def project_qk_early(s):
+            q_part = [held.tile([P, T], F32, name=f"q_part{s}_{m}") for m in range(NB)]
+            k_part = [held.tile([P, T], F32, name=f"k_part{s}_{m}") for m in range(NB)]
+            for m in range(NB):
+                q_acc, k_acc = sum_qk(s, m, EARLY)
+                nc.scalar.activation(q_part[m][:], q_acc[:], FUNC.Identity, bias=bq_sb[:, m : m + 1])
+                nc.scalar.copy(k_part[m][:], k_acc[:])
+            return q_part, k_part
 
-            if by_table_block:
-                all_sums = [new_sums(m) for m in range(NB)]
-                for d in range(NB):
-                    for m in range(NB):
-                        add_block(all_sums[m], m, d)
-                for m in range(NB):
-                    store(all_sums[m], m)
-            else:
-                for m in range(NB):
-                    sums = new_sums(m)
-                    for d in range(NB):
-                        add_block(sums, m, d)
-                    store(sums, m)
+        def project_qk_late(s, q_part, k_part):
+            q_bf = [pair.tile([P, T], BF16, name=f"q{m}") for m in range(NB)]
+            k_bf = [pair.tile([P, T], BF16, name=f"k{m}") for m in range(NB)]
+            for m in range(NB):
+                q_acc, k_acc = sum_qk(s, m, LATE)
+                nc.vector.tensor_tensor(q_bf[m][:], q_acc[:], q_part[m][:], ADD)
+                nc.vector.tensor_tensor(k_bf[m][:], k_acc[:], k_part[m][:], ADD)
             return q_bf, k_bf
 
         def project_v(s):
@@ -147,11 +142,17 @@ def tile_attentionwithpositionalencoding_b_kernel(tc, table, pe, wq, bq, wk, wv,
                 nc.scalar.copy(out_sb[:], mixed[:])
                 nc.sync.dma_start(out[block(m), s * T : (s + 1) * T], out_sb[:])
 
-        q_bf, k_bf = project_qk(0, by_table_block=True)
+        for d in EARLY:
+            embed(d)
+        parked = [project_qk_early(s) for s in range(B)]
+        for d in LATE:
+            embed(d)
+
+        q_bf, k_bf = project_qk_late(0, parked[0][0], parked[0][1])
         for s in range(B):
             a_bf = attention_weights(q_bf, k_bf)
             vt_bf = project_v(s)
             if s + 1 < B:
-                q_bf, k_bf = project_qk(s + 1, by_table_block=False)
+                q_bf, k_bf = project_qk_late(s + 1, parked[s + 1][0], parked[s + 1][1])
             at_bf = flip(a_bf)
             attend(s, vt_bf, at_bf)

@@ -61,67 +61,78 @@ def tile_attentionwithpositionalencoding_b_kernel(tc, table, pe, wq, bq, wk, wv,
 
         e_bf = [[held.tile([P, T], BF16, name=f"e{d}_{s}") for s in range(B)] for d in range(NB)]
 
-        def embed(d):
-            for s in range(B):
-                e32 = pair.tile([P, T], F32, name="e32")
-                picked = table_sb[d][:].indirect(offsets[:, s * (T // 16) : (s + 1) * (T // 16)])
-                nc.vector.tensor_tensor(e32[:], picked, pe_sb[d][:], ADD)
-                nc.vector.tensor_copy(e_bf[d][s][:], e32[:])
+        def embed(d, s):
+            e32 = pair.tile([P, T], F32, name="e32")
+            picked = table_sb[d][:].indirect(offsets[:, s * (T // 16) : (s + 1) * (T // 16)])
+            nc.vector.tensor_tensor(e32[:], picked, pe_sb[d][:], ADD)
+            nc.vector.tensor_copy(e_bf[d][s][:], e32[:])
 
-        def sum_qk(s, m, blocks):
-            q_acc = psum.tile([P, T], F32, name="q_acc", tag="bank")
-            k_acc = psum.tile([P, T], F32, name="k_acc", tag="bank")
-            for d in blocks:
-                first, last = d == blocks[0], d == blocks[-1]
-                nc.tensor.matmul(q_acc[:], wq_sb[d][:, block(m)], e_bf[d][s][:], start=first, stop=last)
-                nc.tensor.matmul(k_acc[:], wk_sb[d][:, block(m)], e_bf[d][s][:], start=first, stop=last)
-            return q_acc, k_acc
+        def add_qk(s, m, d, blocks, sums):
+            if d == blocks[0]:
+                q_acc = psum.tile([P, T], F32, name="q_acc", tag="bank")
+                k_acc = psum.tile([P, T], F32, name="k_acc", tag="bank")
+                sums[m] = (q_acc, k_acc)
+            q_acc, k_acc = sums[m]
+            first, last = d == blocks[0], d == blocks[-1]
+            nc.tensor.matmul(q_acc[:], wq_sb[d][:, block(m)], e_bf[d][s][:], start=first, stop=last)
+            nc.tensor.matmul(k_acc[:], wk_sb[d][:, block(m)], e_bf[d][s][:], start=first, stop=last)
 
-        def project_qk_early(s):
+        def project_qk_early(s, block_by_block):
             q_part = [held.tile([P, T], F32, name=f"q_part{s}_{m}") for m in range(NB)]
             k_part = [held.tile([P, T], F32, name=f"k_part{s}_{m}") for m in range(NB)]
-            for m in range(NB):
-                q_acc, k_acc = sum_qk(s, m, EARLY)
-                nc.scalar.activation(q_part[m][:], q_acc[:], FUNC.Identity, bias=bq_sb[:, m : m + 1])
-                nc.scalar.copy(k_part[m][:], k_acc[:])
+            if block_by_block:
+                order = [(d, m) for d in EARLY for m in range(NB)]
+            else:
+                order = [(d, m) for m in range(NB) for d in EARLY]
+            sums = {}
+            for d, m in order:
+                add_qk(s, m, d, EARLY, sums)
+                if d == EARLY[-1]:
+                    q_acc, k_acc = sums[m]
+                    nc.scalar.activation(q_part[m][:], q_acc[:], FUNC.Identity, bias=bq_sb[:, m : m + 1])
+                    nc.scalar.copy(k_part[m][:], k_acc[:])
             return q_part, k_part
 
-        def project_qk_late(s, q_part, k_part):
+        def project_qk_late(s, parts):
+            q_part, k_part = parts
             q_bf = [pair.tile([P, T], BF16, name=f"q{m}") for m in range(NB)]
             k_bf = [pair.tile([P, T], BF16, name=f"k{m}") for m in range(NB)]
+            sums = {}
             for m in range(NB):
-                q_acc, k_acc = sum_qk(s, m, LATE)
+                for d in LATE:
+                    add_qk(s, m, d, LATE, sums)
+                q_acc, k_acc = sums[m]
                 nc.vector.tensor_tensor(q_bf[m][:], q_acc[:], q_part[m][:], ADD)
                 nc.vector.tensor_tensor(k_bf[m][:], k_acc[:], k_part[m][:], ADD)
             return q_bf, k_bf
 
-        def project_v(s):
-            vt_bf = [pair.tile([P, D], BF16, name=f"vt{j}") for j in range(NB)]
-            for j in range(NB):
-                acc = psum.tile([P, D], F32, name="acc", tag="bank")
-                for d in range(NB):
-                    nc.tensor.matmul(acc[:], e_bf[d][s][:, block(j)], wv_sb[d][:], start=(d == 0), stop=(d == NB - 1))
-                nc.vector.tensor_tensor(vt_bf[j][:], acc[:], bv_all[:], ADD)
-            return vt_bf
+        def project_v(s, j, vt_bf):
+            acc = psum.tile([P, D], F32, name="acc", tag="bank")
+            for d in range(NB):
+                nc.tensor.matmul(acc[:], e_bf[d][s][:, block(j)], wv_sb[d][:], start=(d == 0), stop=(d == NB - 1))
+            nc.vector.tensor_tensor(vt_bf[j][:], acc[:], bv_all[:], ADD)
 
         def attention_weights(q_bf, k_bf):
-            a_bf = []
-            for i in range(NB):
-                score = psum.tile([P, T], F32, name="score", tag="bank")
-                for m in range(NB):
-                    nc.tensor.matmul(score[:], q_bf[m][:, block(i)], k_bf[m][:], start=(m == 0), stop=(m == NB - 1))
-                top = many.tile([P, 1], F32, name="top")
-                nc.vector.reduce_max(top[:], score[:], axis=mybir.AxisListType.X)
-                shift = many.tile([P, 1], F32, name="shift")
-                nc.vector.tensor_scalar_mul(shift[:], top[:], -SCALE)
-                grown = ring.tile([P, T], F32, name="grown")
-                total = many.tile([P, 1], F32, name="total")
-                nc.scalar.activation(grown[:], score[:], FUNC.Exp, bias=shift[:], scale=SCALE, accum_out=total[:])
-                share = many.tile([P, 1], F32, name="share")
-                nc.vector.reciprocal(share[:], total[:])
-                a_i = many.tile([P, T], BF16, name="a_i")
-                nc.vector.tensor_scalar_mul(a_i[:], grown[:], share[:])
-                a_bf.append(a_i)
+            grown, total, a_bf = [], [], []
+            for i in range(NB + 1):
+                if i < NB:
+                    score = psum.tile([P, T], F32, name="score", tag="bank")
+                    for m in range(NB):
+                        nc.tensor.matmul(score[:], q_bf[m][:, block(i)], k_bf[m][:], start=(m == 0), stop=(m == NB - 1))
+                    top = many.tile([P, 1], F32, name="top")
+                    nc.vector.reduce_max(top[:], score[:], axis=mybir.AxisListType.X)
+                    shift = many.tile([P, 1], F32, name="shift")
+                    nc.vector.tensor_scalar_mul(shift[:], top[:], -SCALE)
+                    grown.append(ring.tile([P, T], F32, name="grown"))
+                    total.append(many.tile([P, 1], F32, name="total"))
+                    nc.scalar.activation(
+                        grown[i][:], score[:], FUNC.Exp, bias=shift[:], scale=SCALE, accum_out=total[i][:]
+                    )
+                if i > 0:
+                    share = many.tile([P, 1], F32, name="share")
+                    nc.vector.reciprocal(share[:], total[i - 1][:])
+                    a_bf.append(many.tile([P, T], BF16, name="a_i"))
+                    nc.vector.tensor_scalar_mul(a_bf[i - 1][:], grown[i - 1][:], share[:])
             return a_bf
 
         def flip(a_bf):
@@ -143,16 +154,21 @@ def tile_attentionwithpositionalencoding_b_kernel(tc, table, pe, wq, bq, wk, wv,
                 nc.sync.dma_start(out[block(m), s * T : (s + 1) * T], out_sb[:])
 
         for d in EARLY:
-            embed(d)
-        parked = [project_qk_early(s) for s in range(B)]
+            for s in range(B):
+                embed(d, s)
+        parked = [project_qk_early(s, block_by_block=(s == 0)) for s in range(B)]
         for d in LATE:
-            embed(d)
+            for s in range(B):
+                embed(d, s)
+        q_bf, k_bf = project_qk_late(0, parked[0])
 
-        q_bf, k_bf = project_qk_late(0, parked[0][0], parked[0][1])
         for s in range(B):
             a_bf = attention_weights(q_bf, k_bf)
-            vt_bf = project_v(s)
-            if s + 1 < B:
-                q_bf, k_bf = project_qk_late(s + 1, parked[s + 1][0], parked[s + 1][1])
+            vt_bf = [pair.tile([P, D], BF16, name=f"vt{j}") for j in range(NB)]
+            for j in range(NB - 1):
+                project_v(s, j, vt_bf)
             at_bf = flip(a_bf)
+            project_v(s, NB - 1, vt_bf)
+            if s + 1 < B:
+                q_bf, k_bf = project_qk_late(s + 1, parked[s + 1])
             attend(s, vt_bf, at_bf)

@@ -65,7 +65,10 @@ def tile_attentionwithpositionalencoding_b_kernel(tc, table, pe, wq, bq, wk, wv,
             e32 = pair.tile([P, T], F32, name="e32")
             picked = table_sb[d][:].indirect(offsets[:, s * (T // 16) : (s + 1) * (T // 16)])
             nc.vector.tensor_tensor(e32[:], picked, pe_sb[d][:], ADD)
-            nc.vector.tensor_copy(e_bf[d][s][:], e32[:])
+            if d in EARLY:
+                nc.scalar.copy(e_bf[d][s][:], e32[:])
+            else:
+                nc.vector.tensor_copy(e_bf[d][s][:], e32[:])
 
         def add_qk(s, m, d, blocks, sums):
             if d == blocks[0]:

@@ -11,8 +11,15 @@ B = 4
 T = 512
 NB = D // P
 assert T // P == NB
-EARLY = (0, 1)
-LATE = (2, 3)
+
+
+def early_blocks(s):
+    return (0,) if s == B - 1 else (0, 1)
+
+
+def late_blocks(s):
+    return tuple(d for d in range(NB) if d not in early_blocks(s))
+
 
 F32 = mybir.dt.float32
 BF16 = mybir.dt.bfloat16
@@ -65,10 +72,7 @@ def tile_attentionwithpositionalencoding_b_kernel(tc, table, pe, wq, bq, wk, wv,
             e32 = pair.tile([P, T], F32, name="e32")
             picked = table_sb[d][:].indirect(offsets[:, s * (T // 16) : (s + 1) * (T // 16)])
             nc.vector.tensor_tensor(e32[:], picked, pe_sb[d][:], ADD)
-            if d in EARLY:
-                nc.scalar.copy(e_bf[d][s][:], e32[:])
-            else:
-                nc.vector.tensor_copy(e_bf[d][s][:], e32[:])
+            nc.vector.tensor_copy(e_bf[d][s][:], e32[:])
 
         def add_qk(s, m, d, blocks, sums):
             if d == blocks[0]:
@@ -83,14 +87,15 @@ def tile_attentionwithpositionalencoding_b_kernel(tc, table, pe, wq, bq, wk, wv,
         def project_qk_early(s, block_by_block):
             q_part = [held.tile([P, T], F32, name=f"q_part{s}_{m}") for m in range(NB)]
             k_part = [held.tile([P, T], F32, name=f"k_part{s}_{m}") for m in range(NB)]
+            blocks = early_blocks(s)
             if block_by_block:
-                order = [(d, m) for d in EARLY for m in range(NB)]
+                order = [(d, m) for d in blocks for m in range(NB)]
             else:
-                order = [(d, m) for m in range(NB) for d in EARLY]
+                order = [(d, m) for m in range(NB) for d in blocks]
             sums = {}
             for d, m in order:
-                add_qk(s, m, d, EARLY, sums)
-                if d == EARLY[-1]:
+                add_qk(s, m, d, blocks, sums)
+                if d == blocks[-1]:
                     q_acc, k_acc = sums[m]
                     nc.scalar.activation(q_part[m][:], q_acc[:], FUNC.Identity, bias=bq_sb[:, m : m + 1])
                     nc.scalar.copy(k_part[m][:], k_acc[:])
@@ -100,10 +105,11 @@ def tile_attentionwithpositionalencoding_b_kernel(tc, table, pe, wq, bq, wk, wv,
             q_part, k_part = parts
             q_bf = [pair.tile([P, T], BF16, name=f"q{m}") for m in range(NB)]
             k_bf = [pair.tile([P, T], BF16, name=f"k{m}") for m in range(NB)]
+            blocks = late_blocks(s)
             sums = {}
             for m in range(NB):
-                for d in LATE:
-                    add_qk(s, m, d, LATE, sums)
+                for d in blocks:
+                    add_qk(s, m, d, blocks, sums)
                 q_acc, k_acc = sums[m]
                 nc.vector.tensor_tensor(q_bf[m][:], q_acc[:], q_part[m][:], ADD)
                 nc.vector.tensor_tensor(k_bf[m][:], k_acc[:], k_part[m][:], ADD)
@@ -156,11 +162,15 @@ def tile_attentionwithpositionalencoding_b_kernel(tc, table, pe, wq, bq, wk, wv,
                 nc.scalar.copy(out_sb[:], mixed[:])
                 nc.sync.dma_start(out[block(m), s * T : (s + 1) * T], out_sb[:])
 
-        for d in EARLY:
-            for s in range(B):
-                embed(d, s)
-        parked = [project_qk_early(s, block_by_block=(s == 0)) for s in range(B)]
-        for d in LATE:
+        last_first = [B - 1] + list(range(B - 1))
+        for s in last_first:
+            embed(0, s)
+        for s in range(B):
+            embed(1, s)
+        parked = {}
+        for s in last_first:
+            parked[s] = project_qk_early(s, block_by_block=(s == 0))
+        for d in (2, 3):
             for s in range(B):
                 embed(d, s)
         q_bf, k_bf = project_qk_late(0, parked[0])

@@ -74,15 +74,30 @@ def tile_attentionwithpositionalencoding_b_kernel(tc, table, pe, wq, bq, wk, wv,
             nc.vector.tensor_tensor(e32[:], picked, pe_sb[d][:], ADD)
             nc.vector.tensor_copy(e_bf[d][s][:], e32[:])
 
-        def add_qk(s, m, d, blocks, sums):
+        def open_turn(a_bf, i):
+            return (a_bf[i], psum.tile([P, NB, P], BF16, name="flipped", tag="bank"))
+
+        def turn_step(turn, j):
+            if turn is not None and j < NB:
+                a_i, flipped = turn
+                nc.tensor.transpose(flipped[:, j, :], a_i[:, block(j)], ident[:])
+
+        def close_turn(turn, at_bf, i):
+            if turn is not None:
+                nc.vector.tensor_copy(at_bf[:, :, block(i)], turn[1][:])
+
+        def add_qk(s, m, d, blocks, sums, turn=None):
             if d == blocks[0]:
                 q_acc = psum.tile([P, T], F32, name="q_acc", tag="bank")
                 k_acc = psum.tile([P, T], F32, name="k_acc", tag="bank")
                 sums[m] = (q_acc, k_acc)
             q_acc, k_acc = sums[m]
             first, last = d == blocks[0], d == blocks[-1]
+            n = blocks.index(d)
             nc.tensor.matmul(q_acc[:], wq_sb[d][:, block(m)], e_bf[d][s][:], start=first, stop=last)
+            turn_step(turn, 2 * n)
             nc.tensor.matmul(k_acc[:], wk_sb[d][:, block(m)], e_bf[d][s][:], start=first, stop=last)
+            turn_step(turn, 2 * n + 1)
 
         def project_qk_early(s, block_by_block):
             q_part = [held.tile([P, T], F32, name=f"q_part{s}_{m}") for m in range(NB)]
@@ -101,24 +116,28 @@ def tile_attentionwithpositionalencoding_b_kernel(tc, table, pe, wq, bq, wk, wv,
                     nc.scalar.copy(k_part[m][:], k_acc[:])
             return q_part, k_part
 
-        def project_qk_late(s, parts):
+        def project_qk_late(s, parts, a_bf=None, at_bf=None):
             q_part, k_part = parts
             q_bf = [pair.tile([P, T], BF16, name=f"q{m}") for m in range(NB)]
             k_bf = [pair.tile([P, T], BF16, name=f"k{m}") for m in range(NB)]
             blocks = late_blocks(s)
             sums = {}
             for m in range(NB):
+                i = m + NB // 2
+                turn = open_turn(a_bf, i) if a_bf is not None and i < NB else None
                 for d in blocks:
-                    add_qk(s, m, d, blocks, sums)
+                    add_qk(s, m, d, blocks, sums, turn)
                 q_acc, k_acc = sums[m]
                 nc.vector.tensor_tensor(q_bf[m][:], q_acc[:], q_part[m][:], ADD)
                 nc.vector.tensor_tensor(k_bf[m][:], k_acc[:], k_part[m][:], ADD)
+                close_turn(turn, at_bf, i)
             return q_bf, k_bf
 
-        def project_v(s, j, vt_bf):
+        def project_v(s, j, vt_bf, turn=None):
             acc = psum.tile([P, D], F32, name="acc", tag="bank")
             for d in range(NB):
                 nc.tensor.matmul(acc[:], e_bf[d][s][:, block(j)], wv_sb[d][:], start=(d == 0), stop=(d == NB - 1))
+                turn_step(turn, d)
             nc.vector.tensor_tensor(vt_bf[j][:], acc[:], bv_all[:], ADD)
 
         def attention_weights(q_bf, k_bf):
@@ -143,15 +162,6 @@ def tile_attentionwithpositionalencoding_b_kernel(tc, table, pe, wq, bq, wk, wv,
                     a_bf.append(many.tile([P, T], BF16, name="a_i"))
                     nc.vector.tensor_scalar_mul(a_bf[i - 1][:], grown[i - 1][:], share[:])
             return a_bf
-
-        def flip(a_bf):
-            at_bf = pair.tile([P, NB, T], BF16, name="at_bf")
-            for i in range(NB):
-                flipped = psum.tile([P, NB, P], BF16, name="flipped", tag="bank")
-                for j in range(NB):
-                    nc.tensor.transpose(flipped[:, j, :], a_bf[i][:, block(j)], ident[:])
-                nc.vector.tensor_copy(at_bf[:, :, block(i)], flipped[:])
-            return at_bf
 
         def attend(s, vt_bf, at_bf):
             for m in range(NB):
@@ -178,10 +188,12 @@ def tile_attentionwithpositionalencoding_b_kernel(tc, table, pe, wq, bq, wk, wv,
         for s in range(B):
             a_bf = attention_weights(q_bf, k_bf)
             vt_bf = [pair.tile([P, D], BF16, name=f"vt{j}") for j in range(NB)]
-            for j in range(NB - 1):
-                project_v(s, j, vt_bf)
-            at_bf = flip(a_bf)
-            project_v(s, NB - 1, vt_bf)
+            at_bf = pair.tile([P, NB, T], BF16, name="at_bf")
+            ahead = NB // 2 if s + 1 < B else 0
+            for j in range(NB):
+                turn = open_turn(a_bf, j - ahead) if j >= ahead else None
+                project_v(s, j, vt_bf, turn)
+                close_turn(turn, at_bf, j - ahead)
             if s + 1 < B:
-                q_bf, k_bf = project_qk_late(s + 1, parked[s + 1])
+                q_bf, k_bf = project_qk_late(s + 1, parked[s + 1], a_bf, at_bf)
             attend(s, vt_bf, at_bf)

@@ -163,8 +163,8 @@ def tile_attentionwithpositionalencoding_b_kernel(tc, table, pe, wq, bq, wk, wv,
                     nc.vector.tensor_scalar_mul(a_bf[i - 1][:], grown[i - 1][:], share[:])
             return a_bf
 
-        def attend(s, vt_bf, at_bf):
-            for m in range(NB):
+        def attend(s, vt_bf, at_bf, feature_blocks):
+            for m in feature_blocks:
                 mixed = psum.tile([P, T], F32, name="mixed", tag="bank")
                 for j in range(NB):
                     nc.tensor.matmul(mixed[:], vt_bf[j][:, block(m)], at_bf[:, j, :], start=(j == 0), stop=(j == NB - 1))
@@ -185,6 +185,8 @@ def tile_attentionwithpositionalencoding_b_kernel(tc, table, pe, wq, bq, wk, wv,
                 embed(d, s)
         q_bf, k_bf = project_qk_late(0, parked[0])
 
+        first_half, second_half = range(NB // 2), range(NB // 2, NB)
+        kept_back = None
         for s in range(B):
             a_bf = attention_weights(q_bf, k_bf)
             vt_bf = [pair.tile([P, D], BF16, name=f"vt{j}") for j in range(NB)]
@@ -196,4 +198,10 @@ def tile_attentionwithpositionalencoding_b_kernel(tc, table, pe, wq, bq, wk, wv,
                 close_turn(turn, at_bf, j - ahead)
             if s + 1 < B:
                 q_bf, k_bf = project_qk_late(s + 1, parked[s + 1], a_bf, at_bf)
-            attend(s, vt_bf, at_bf)
+            if kept_back is not None:
+                attend(s - 1, kept_back[0], kept_back[1], second_half)
+            attend(s, vt_bf, at_bf, first_half)
+            if s + 2 == B:
+                kept_back = (vt_bf, at_bf)
+            else:
+                attend(s, vt_bf, at_bf, second_half)

@@ -14,7 +14,11 @@ assert T // P == NB
 
 
 def early_blocks(s):
-    return (0,) if s == B - 1 else (0, 1)
+    if s == B - 1:
+        return (0,)
+    if s == B - 2:
+        return (0, 1, 2)
+    return (0, 1)
 
 
 def late_blocks(s):
@@ -74,30 +78,36 @@ def tile_attentionwithpositionalencoding_b_kernel(tc, table, pe, wq, bq, wk, wv,
             nc.vector.tensor_tensor(e32[:], picked, pe_sb[d][:], ADD)
             nc.vector.tensor_copy(e_bf[d][s][:], e32[:])
 
-        def open_turn(a_bf, i):
-            return (a_bf[i], psum.tile([P, NB, P], BF16, name="flipped", tag="bank"))
+        def nothing():
+            pass
 
-        def turn_step(turn, j):
-            if turn is not None and j < NB:
-                a_i, flipped = turn
-                nc.tensor.transpose(flipped[:, j, :], a_i[:, block(j)], ident[:])
+        def transposer(a_bf, at_bf):
+            todo = [(i, j) for i in range(NB) for j in range(NB)]
+            banks = []
 
-        def close_turn(turn, at_bf, i):
-            if turn is not None:
-                nc.vector.tensor_copy(at_bf[:, :, block(i)], turn[1][:])
+            def carry():
+                if todo:
+                    i, j = todo[0]
+                    todo.remove((i, j))
+                    if j == 0:
+                        banks.append(psum.tile([P, NB, P], BF16, name="flipped", tag="bank"))
+                    nc.tensor.transpose(banks[i][:, j, :], a_bf[i][:, block(j)], ident[:])
+                    if j == NB - 1:
+                        nc.vector.tensor_copy(at_bf[:, :, block(i)], banks[i][:])
 
-        def add_qk(s, m, d, blocks, sums, turn=None):
+            return carry
+
+        def add_qk(s, m, d, blocks, sums, carry):
             if d == blocks[0]:
                 q_acc = psum.tile([P, T], F32, name="q_acc", tag="bank")
                 k_acc = psum.tile([P, T], F32, name="k_acc", tag="bank")
                 sums[m] = (q_acc, k_acc)
             q_acc, k_acc = sums[m]
             first, last = d == blocks[0], d == blocks[-1]
-            n = blocks.index(d)
             nc.tensor.matmul(q_acc[:], wq_sb[d][:, block(m)], e_bf[d][s][:], start=first, stop=last)
-            turn_step(turn, 2 * n)
+            carry()
             nc.tensor.matmul(k_acc[:], wk_sb[d][:, block(m)], e_bf[d][s][:], start=first, stop=last)
-            turn_step(turn, 2 * n + 1)
+            carry()
 
         def project_qk_early(s, block_by_block):
             q_part = [held.tile([P, T], F32, name=f"q_part{s}_{m}") for m in range(NB)]
@@ -109,35 +119,32 @@ def tile_attentionwithpositionalencoding_b_kernel(tc, table, pe, wq, bq, wk, wv,
                 order = [(d, m) for m in range(NB) for d in blocks]
             sums = {}
             for d, m in order:
-                add_qk(s, m, d, blocks, sums)
+                add_qk(s, m, d, blocks, sums, nothing)
                 if d == blocks[-1]:
                     q_acc, k_acc = sums[m]
                     nc.scalar.activation(q_part[m][:], q_acc[:], FUNC.Identity, bias=bq_sb[:, m : m + 1])
                     nc.scalar.copy(k_part[m][:], k_acc[:])
             return q_part, k_part
 
-        def project_qk_late(s, parts, a_bf=None, at_bf=None):
+        def project_qk_late(s, parts, carry):
             q_part, k_part = parts
             q_bf = [pair.tile([P, T], BF16, name=f"q{m}") for m in range(NB)]
             k_bf = [pair.tile([P, T], BF16, name=f"k{m}") for m in range(NB)]
             blocks = late_blocks(s)
             sums = {}
             for m in range(NB):
-                i = m + NB // 2
-                turn = open_turn(a_bf, i) if a_bf is not None and i < NB else None
                 for d in blocks:
-                    add_qk(s, m, d, blocks, sums, turn)
+                    add_qk(s, m, d, blocks, sums, carry)
                 q_acc, k_acc = sums[m]
                 nc.vector.tensor_tensor(q_bf[m][:], q_acc[:], q_part[m][:], ADD)
                 nc.vector.tensor_tensor(k_bf[m][:], k_acc[:], k_part[m][:], ADD)
-                close_turn(turn, at_bf, i)
             return q_bf, k_bf
 
-        def project_v(s, j, vt_bf, turn=None):
+        def project_v(s, j, vt_bf, carry):
             acc = psum.tile([P, D], F32, name="acc", tag="bank")
             for d in range(NB):
                 nc.tensor.matmul(acc[:], e_bf[d][s][:, block(j)], wv_sb[d][:], start=(d == 0), stop=(d == NB - 1))
-                turn_step(turn, d)
+                carry()
             nc.vector.tensor_tensor(vt_bf[j][:], acc[:], bv_all[:], ADD)
 
         def attention_weights(q_bf, k_bf):
@@ -163,14 +170,20 @@ def tile_attentionwithpositionalencoding_b_kernel(tc, table, pe, wq, bq, wk, wv,
                     nc.vector.tensor_scalar_mul(a_bf[i - 1][:], grown[i - 1][:], share[:])
             return a_bf
 
-        def attend(s, vt_bf, at_bf, feature_blocks):
+        def attend(s, vt_bf, at_bf, feature_blocks, carry, pieces=1):
+            width = T // pieces
             for m in feature_blocks:
-                mixed = psum.tile([P, T], F32, name="mixed", tag="bank")
-                for j in range(NB):
-                    nc.tensor.matmul(mixed[:], vt_bf[j][:, block(m)], at_bf[:, j, :], start=(j == 0), stop=(j == NB - 1))
                 out_sb = ring.tile([P, T], F32, name="out_sb")
-                nc.scalar.copy(out_sb[:], mixed[:])
-                nc.sync.dma_start(out[block(m), s * T : (s + 1) * T], out_sb[:])
+                for c in range(pieces):
+                    queries = slice(c * width, (c + 1) * width)
+                    mixed = psum.tile([P, T], F32, name="mixed", tag="bank")
+                    for j in range(NB):
+                        nc.tensor.matmul(
+                            mixed[:, :width], vt_bf[j][:, block(m)], at_bf[:, j, queries], start=(j == 0), stop=(j == NB - 1)
+                        )
+                        carry()
+                    nc.scalar.copy(out_sb[:, queries], mixed[:, :width])
+                    nc.sync.dma_start(out[block(m), s * T + c * width : s * T + (c + 1) * width], out_sb[:, queries])
 
         last_first = [B - 1] + list(range(B - 1))
         for s in last_first:
@@ -178,12 +191,14 @@ def tile_attentionwithpositionalencoding_b_kernel(tc, table, pe, wq, bq, wk, wv,
         for s in range(B):
             embed(1, s)
         parked = {}
-        for s in last_first:
+        for s in last_first[:-1]:
             parked[s] = project_qk_early(s, block_by_block=(s == 0))
-        for d in (2, 3):
-            for s in range(B):
-                embed(d, s)
-        q_bf, k_bf = project_qk_late(0, parked[0])
+        for s in reversed(last_first):
+            embed(2, s)
+        parked[B - 2] = project_qk_early(B - 2, block_by_block=False)
+        for s in range(B):
+            embed(3, s)
+        q_bf, k_bf = project_qk_late(0, parked[0], nothing)
 
         first_half, second_half = range(NB // 2), range(NB // 2, NB)
         kept_back = None
@@ -191,17 +206,18 @@ def tile_attentionwithpositionalencoding_b_kernel(tc, table, pe, wq, bq, wk, wv,
             a_bf = attention_weights(q_bf, k_bf)
             vt_bf = [pair.tile([P, D], BF16, name=f"vt{j}") for j in range(NB)]
             at_bf = pair.tile([P, NB, T], BF16, name="at_bf")
-            ahead = NB // 2 if s + 1 < B else 0
+            carry = transposer(a_bf, at_bf)
             for j in range(NB):
-                turn = open_turn(a_bf, j - ahead) if j >= ahead else None
-                project_v(s, j, vt_bf, turn)
-                close_turn(turn, at_bf, j - ahead)
+                project_v(s, j, vt_bf, nothing if s == 0 and j < NB // 2 else carry)
             if s + 1 < B:
-                q_bf, k_bf = project_qk_late(s + 1, parked[s + 1], a_bf, at_bf)
+                q_bf, k_bf = project_qk_late(s + 1, parked[s + 1], carry)
             if kept_back is not None:
-                attend(s - 1, kept_back[0], kept_back[1], second_half)
-            attend(s, vt_bf, at_bf, first_half)
+                attend(s - 1, kept_back[0], kept_back[1], second_half, carry)
+            attend(s, vt_bf, at_bf, first_half, nothing)
             if s + 2 == B:
                 kept_back = (vt_bf, at_bf)
+            elif s + 1 < B:
+                attend(s, vt_bf, at_bf, second_half, nothing)
             else:
-                attend(s, vt_bf, at_bf, second_half)
+                attend(s, vt_bf, at_bf, second_half[:1], nothing)
+                attend(s, vt_bf, at_bf, second_half[1:], nothing, pieces=4)

@@ -93,7 +93,7 @@ def tile_attentionwithpositionalencoding_b_kernel(tc, table, pe, wq, bq, wk, wv,
                         banks.append(psum.tile([P, NB, P], BF16, name="flipped", tag="bank"))
                     nc.tensor.transpose(banks[i][:, j, :], a_bf[i][:, block(j)], ident[:])
                     if j == NB - 1:
-                        nc.vector.tensor_copy(at_bf[:, :, block(i)], banks[i][:])
+                        nc.scalar.copy(at_bf[:, :, block(i)], banks[i][:])
 
             return carry
 

@@ -201,9 +201,11 @@ def tile_attentionwithpositionalencoding_b_kernel(tc, table, pe, wq, bq, wk, wv,
         q_bf, k_bf = project_qk_late(0, parked[0], nothing)
 
         first_half, second_half = range(NB // 2), range(NB // 2, NB)
-        kept_back = None
         for s in range(B):
             a_bf = attention_weights(q_bf, k_bf)
+            if 0 < s < B - 1:
+                attend(s - 1, vt_bf, at_bf, second_half, nothing)
+            before = (vt_bf, at_bf) if s == B - 1 else None
             vt_bf = [pair.tile([P, D], BF16, name=f"vt{j}") for j in range(NB)]
             at_bf = pair.tile([P, NB, T], BF16, name="at_bf")
             carry = transposer(a_bf, at_bf)
@@ -211,13 +213,8 @@ def tile_attentionwithpositionalencoding_b_kernel(tc, table, pe, wq, bq, wk, wv,
                 project_v(s, j, vt_bf, nothing if s == 0 and j < NB // 2 else carry)
             if s + 1 < B:
                 q_bf, k_bf = project_qk_late(s + 1, parked[s + 1], carry)
-            if kept_back is not None:
-                attend(s - 1, kept_back[0], kept_back[1], second_half, carry)
-            attend(s, vt_bf, at_bf, first_half, nothing)
-            if s + 2 == B:
-                kept_back = (vt_bf, at_bf)
-            elif s + 1 < B:
-                attend(s, vt_bf, at_bf, second_half, nothing)
             else:
-                attend(s, vt_bf, at_bf, second_half[:1], nothing)
-                attend(s, vt_bf, at_bf, second_half[1:], nothing, pieces=4)
+                attend(s - 1, before[0], before[1], second_half, carry)
+            attend(s, vt_bf, at_bf, first_half, nothing)
+        attend(B - 1, vt_bf, at_bf, second_half[:1], nothing)
+        attend(B - 1, vt_bf, at_bf, second_half[1:], nothing, pieces=4)

@@ -78,7 +78,7 @@ def tile_attentionwithpositionalencoding_b_kernel(tc, table, pe, wq, bq, wk, wv,
             nc.vector.tensor_tensor(e32[:], picked, pe_sb[d][:], ADD)
             nc.vector.tensor_copy(e_bf[d][s][:], e32[:])
 
-        def nothing():
+        def nothing(*unused):
             pass
 
         def transposer(a_bf, at_bf):
@@ -126,7 +126,7 @@ def tile_attentionwithpositionalencoding_b_kernel(tc, table, pe, wq, bq, wk, wv,
                     nc.scalar.copy(k_part[m][:], k_acc[:])
             return q_part, k_part
 
-        def project_qk_late(s, parts, carry):
+        def project_qk_late(s, parts, carry, after_block):
             q_part, k_part = parts
             q_bf = [pair.tile([P, T], BF16, name=f"q{m}") for m in range(NB)]
             k_bf = [pair.tile([P, T], BF16, name=f"k{m}") for m in range(NB)]
@@ -138,6 +138,7 @@ def tile_attentionwithpositionalencoding_b_kernel(tc, table, pe, wq, bq, wk, wv,
                 q_acc, k_acc = sums[m]
                 nc.vector.tensor_tensor(q_bf[m][:], q_acc[:], q_part[m][:], ADD)
                 nc.vector.tensor_tensor(k_bf[m][:], k_acc[:], k_part[m][:], ADD)
+                after_block(m)
             return q_bf, k_bf
 
         def project_v(s, j, vt_bf, carry):
@@ -198,23 +199,28 @@ def tile_attentionwithpositionalencoding_b_kernel(tc, table, pe, wq, bq, wk, wv,
         parked[B - 2] = project_qk_early(B - 2, block_by_block=False)
         for s in range(B):
             embed(3, s)
-        q_bf, k_bf = project_qk_late(0, parked[0], nothing)
+        q_bf, k_bf = project_qk_late(0, parked[0], nothing, nothing)
 
         first_half, second_half = range(NB // 2), range(NB // 2, NB)
+        before = None
         for s in range(B):
             a_bf = attention_weights(q_bf, k_bf)
-            if 0 < s < B - 1:
-                attend(s - 1, vt_bf, at_bf, second_half, nothing)
-            before = (vt_bf, at_bf) if s == B - 1 else None
             vt_bf = [pair.tile([P, D], BF16, name=f"vt{j}") for j in range(NB)]
             at_bf = pair.tile([P, NB, T], BF16, name="at_bf")
             carry = transposer(a_bf, at_bf)
             for j in range(NB):
                 project_v(s, j, vt_bf, nothing if s == 0 and j < NB // 2 else carry)
+
+            def kept_back(m):
+                if before is not None and m < len(second_half):
+                    attend(s - 1, before[0], before[1], second_half[m : m + 1], carry)
+
             if s + 1 < B:
-                q_bf, k_bf = project_qk_late(s + 1, parked[s + 1], carry)
+                q_bf, k_bf = project_qk_late(s + 1, parked[s + 1], carry, kept_back)
             else:
-                attend(s - 1, before[0], before[1], second_half, carry)
+                for m in range(NB):
+                    kept_back(m)
             attend(s, vt_bf, at_bf, first_half, nothing)
+            before = (vt_bf, at_bf)
         attend(B - 1, vt_bf, at_bf, second_half[:1], nothing)
         attend(B - 1, vt_bf, at_bf, second_half[1:], nothing, pieces=4)

@@ -60,13 +60,13 @@ def tile_attentionwithpositionalencoding_b_kernel(tc, table, pe, wq, bq, wk, wv,
             nc.sync.dma_start(table_sb[d][:], table[block(d), :])
             nc.sync.dma_start(wq_sb[d][:], wq[block(d), :])
             nc.sync.dma_start(wk_sb[d][:], wk[block(d), :])
+        bq_sb = held.tile([P, NB], F32, name="bq_sb")
+        with nc.allow_non_contiguous_dma(reason="512 biases, one to a partition"):
+            nc.sync.dma_start(bq_sb[:], bq.rearrange("(m p) o -> p (m o)", p=P))
         for d in range(NB):
             nc.sync.dma_start(wv_sb[d][:], wv[block(d), :])
         bv_all = held.tile([P, D], F32, name="bv_all")
         nc.sync.dma_start(bv_all[:], bv.rearrange("d o -> (d o)").partition_broadcast(P))
-        bq_sb = held.tile([P, NB], F32, name="bq_sb")
-        with nc.allow_non_contiguous_dma(reason="512 biases, one to a partition"):
-            nc.scalar.dma_start(bq_sb[:], bq.rearrange("(m p) o -> p (m o)", p=P))
         ident = held.tile([P, P], BF16, name="ident")
         make_identity(nc, ident[:])
 
@@ -122,7 +122,7 @@ def tile_attentionwithpositionalencoding_b_kernel(tc, table, pe, wq, bq, wk, wv,
                 add_qk(s, m, d, blocks, sums, nothing)
                 if d == blocks[-1]:
                     q_acc, k_acc = sums[m]
-                    nc.scalar.activation(q_part[m][:], q_acc[:], FUNC.Identity, bias=bq_sb[:, m : m + 1])
+                    nc.scalar.copy(q_part[m][:], q_acc[:])
                     nc.scalar.copy(k_part[m][:], k_acc[:])
             return q_part, k_part
 
@@ -136,7 +136,7 @@ def tile_attentionwithpositionalencoding_b_kernel(tc, table, pe, wq, bq, wk, wv,
                 for d in blocks:
                     add_qk(s, m, d, blocks, sums, carry)
                 q_acc, k_acc = sums[m]
-                nc.vector.tensor_tensor(q_bf[m][:], q_acc[:], q_part[m][:], ADD)
+                nc.vector.scalar_tensor_tensor(q_bf[m][:], q_acc[:], bq_sb[:, m : m + 1], q_part[m][:], ADD, ADD)
                 nc.vector.tensor_tensor(k_bf[m][:], k_acc[:], k_part[m][:], ADD)
                 after_block(m)
             return q_bf, k_bf

@@ -72,11 +72,14 @@ def tile_attentionwithpositionalencoding_b_kernel(tc, table, pe, wq, bq, wk, wv,
 
         e_bf = [[held.tile([P, T], BF16, name=f"e{d}_{s}") for s in range(B)] for d in range(NB)]
 
-        def embed(d, s):
-            e32 = pair.tile([P, T], F32, name="e32")
+        strip = held.tile([P, 2 * T], F32, name="strip")
+        LEFT, RIGHT, ACROSS = 0, T, T // 2
+
+        def embed(d, s, start):
+            e32 = strip[:, start : start + T]
             picked = table_sb[d][:].indirect(offsets[:, s * (T // 16) : (s + 1) * (T // 16)])
-            nc.vector.tensor_tensor(e32[:], picked, pe_sb[d][:], ADD)
-            nc.vector.tensor_copy(e_bf[d][s][:], e32[:])
+            nc.vector.tensor_tensor(e32, picked, pe_sb[d][:], ADD)
+            nc.vector.tensor_copy(e_bf[d][s][:], e32)
 
         def nothing(*unused):
             pass
@@ -187,18 +190,23 @@ def tile_attentionwithpositionalencoding_b_kernel(tc, table, pe, wq, bq, wk, wv,
                     nc.sync.dma_start(out[block(m), s * T + c * width : s * T + (c + 1) * width], out_sb[:, queries])
 
         last_first = [B - 1] + list(range(B - 1))
-        for s in last_first:
-            embed(0, s)
-        for s in range(B):
-            embed(1, s)
+        embed(0, B - 1, ACROSS)
+        embed(0, 0, LEFT)
+        embed(0, 1, RIGHT)
+        embed(1, 0, ACROSS)
+        by_need = [(1, 1), (0, B - 2), (1, B - 2), (2, B - 2), (2, 0), (3, 0)]
+        turns = []
+
+        def embed_in_turn(blocks):
+            for d, s in blocks:
+                embed(d, s, LEFT if len(turns) % 2 == 0 else RIGHT)
+                turns.append((d, s))
+
+        embed_in_turn(by_need + [(d, 1) for d in late_blocks(1)])
         parked = {}
         for s in last_first[:-1]:
             parked[s] = project_qk_early(s, block_by_block=(s == 0))
-        for s in reversed(last_first):
-            embed(2, s)
         parked[B - 2] = project_qk_early(B - 2, block_by_block=False)
-        for s in range(B):
-            embed(3, s)
         q_bf, k_bf = project_qk_late(0, parked[0], nothing, nothing)
 
         first_half, second_half = range(NB // 2), range(NB // 2, NB)
@@ -222,5 +230,7 @@ def tile_attentionwithpositionalencoding_b_kernel(tc, table, pe, wq, bq, wk, wv,
                     kept_back(m)
             attend(s, vt_bf, at_bf, first_half, nothing)
             before = (vt_bf, at_bf)
+            if s + 2 < B:
+                embed_in_turn([(d, s + 2) for d in late_blocks(s + 2)])
         attend(B - 1, vt_bf, at_bf, second_half[:1], nothing)
         attend(B - 1, vt_bf, at_bf, second_half[1:], nothing, pieces=4)

@@ -21,6 +21,10 @@ def early_blocks(s):
     return (0, 1)
 
 
+def kept_open(s):
+    return (NB - 1,) if s == 0 else ()
+
+
 def late_blocks(s):
     return tuple(d for d in range(NB) if d not in early_blocks(s))
 
@@ -100,21 +104,21 @@ def tile_attentionwithpositionalencoding_b_kernel(tc, table, pe, wq, bq, wk, wv,
 
             return carry
 
-        def add_qk(s, m, d, blocks, sums, carry):
-            if d == blocks[0]:
+        def add_qk(s, m, d, last, sums, carry):
+            first = m not in sums
+            if first:
                 q_acc = psum.tile([P, T], F32, name="q_acc", tag="bank")
                 k_acc = psum.tile([P, T], F32, name="k_acc", tag="bank")
                 sums[m] = (q_acc, k_acc)
             q_acc, k_acc = sums[m]
-            first, last = d == blocks[0], d == blocks[-1]
             nc.tensor.matmul(q_acc[:], wq_sb[d][:, block(m)], e_bf[d][s][:], start=first, stop=last)
             carry()
             nc.tensor.matmul(k_acc[:], wk_sb[d][:, block(m)], e_bf[d][s][:], start=first, stop=last)
             carry()
 
         def project_qk_early(s, block_by_block):
-            q_part = [held.tile([P, T], F32, name=f"q_part{s}_{m}") for m in range(NB)]
-            k_part = [held.tile([P, T], F32, name=f"k_part{s}_{m}") for m in range(NB)]
+            q_part = {m: held.tile([P, T], F32, name=f"q_part{s}_{m}") for m in range(NB) if m not in kept_open(s)}
+            k_part = {m: held.tile([P, T], F32, name=f"k_part{s}_{m}") for m in range(NB) if m not in kept_open(s)}
             blocks = early_blocks(s)
             if block_by_block:
                 order = [(d, m) for d in blocks for m in range(NB)]
@@ -122,25 +126,29 @@ def tile_attentionwithpositionalencoding_b_kernel(tc, table, pe, wq, bq, wk, wv,
                 order = [(d, m) for m in range(NB) for d in blocks]
             sums = {}
             for d, m in order:
-                add_qk(s, m, d, blocks, sums, nothing)
-                if d == blocks[-1]:
-                    q_acc, k_acc = sums[m]
+                parks = d == blocks[-1] and m not in kept_open(s)
+                add_qk(s, m, d, parks, sums, nothing)
+                if parks:
+                    q_acc, k_acc = sums.pop(m)
                     nc.scalar.copy(q_part[m][:], q_acc[:])
                     nc.scalar.copy(k_part[m][:], k_acc[:])
-            return q_part, k_part
+            return q_part, k_part, sums
 
         def project_qk_late(s, parts, carry, after_block):
-            q_part, k_part = parts
+            q_part, k_part, sums = parts
             q_bf = [pair.tile([P, T], BF16, name=f"q{m}") for m in range(NB)]
             k_bf = [pair.tile([P, T], BF16, name=f"k{m}") for m in range(NB)]
             blocks = late_blocks(s)
-            sums = {}
             for m in range(NB):
                 for d in blocks:
-                    add_qk(s, m, d, blocks, sums, carry)
+                    add_qk(s, m, d, d == blocks[-1], sums, carry)
                 q_acc, k_acc = sums[m]
-                nc.vector.scalar_tensor_tensor(q_bf[m][:], q_acc[:], bq_sb[:, m : m + 1], q_part[m][:], ADD, ADD)
-                nc.vector.tensor_tensor(k_bf[m][:], k_acc[:], k_part[m][:], ADD)
+                if m in kept_open(s):
+                    nc.scalar.activation(q_bf[m][:], q_acc[:], FUNC.Identity, bias=bq_sb[:, m : m + 1])
+                    nc.scalar.copy(k_bf[m][:], k_acc[:])
+                else:
+                    nc.vector.scalar_tensor_tensor(q_bf[m][:], q_acc[:], bq_sb[:, m : m + 1], q_part[m][:], ADD, ADD)
+                    nc.vector.tensor_tensor(k_bf[m][:], k_acc[:], k_part[m][:], ADD)
                 after_block(m)
             return q_bf, k_bf
 
@@ -174,12 +182,12 @@ def tile_attentionwithpositionalencoding_b_kernel(tc, table, pe, wq, bq, wk, wv,
                     nc.vector.tensor_scalar_mul(a_bf[i - 1][:], grown[i - 1][:], share[:])
             return a_bf
 
-        def attend(s, vt_bf, at_bf, feature_blocks, carry, pieces=1):
-            width = T // pieces
+        def attend(s, vt_bf, at_bf, feature_blocks, carry, ends=(T,)):
             for m in feature_blocks:
                 out_sb = ring.tile([P, T], F32, name="out_sb")
-                for c in range(pieces):
-                    queries = slice(c * width, (c + 1) * width)
+                begin = 0
+                for end in ends:
+                    queries, width = slice(begin, end), end - begin
                     mixed = psum.tile([P, T], F32, name="mixed", tag="bank")
                     for j in range(NB):
                         nc.tensor.matmul(
@@ -187,7 +195,8 @@ def tile_attentionwithpositionalencoding_b_kernel(tc, table, pe, wq, bq, wk, wv,
                         )
                         carry()
                     nc.scalar.copy(out_sb[:, queries], mixed[:, :width])
-                    nc.sync.dma_start(out[block(m), s * T + c * width : s * T + (c + 1) * width], out_sb[:, queries])
+                    nc.sync.dma_start(out[block(m), s * T + begin : s * T + end], out_sb[:, queries])
+                    begin = end
 
         last_first = [B - 1] + list(range(B - 1))
         embed(0, B - 1, ACROSS)
@@ -233,4 +242,4 @@ def tile_attentionwithpositionalencoding_b_kernel(tc, table, pe, wq, bq, wk, wv,
             if s + 2 < B:
                 embed_in_turn([(d, s + 2) for d in late_blocks(s + 2)])
         attend(B - 1, vt_bf, at_bf, second_half[:1], nothing)
-        attend(B - 1, vt_bf, at_bf, second_half[1:], nothing, pieces=4)
+        attend(B - 1, vt_bf, at_bf, second_half[1:], nothing, ends=(3 * T // 4, T))

@@ -22,7 +22,7 @@ def early_blocks(s):
 
 
 def kept_open(s):
-    return (NB - 1,) if s == 0 else ()
+    return (NB - 2, NB - 1) if s == 0 else ()
 
 
 def late_blocks(s):

import math
from contextlib import ExitStack

import concourse.mybir as mybir
from concourse.masks import make_identity

P = 128
D = 512
V = 4096
B = 4
T = 512
NB = D // P
assert T // P == NB


def early_blocks(s):
    if s == B - 1:
        return (0,)
    if s == B - 2:
        return (0, 1, 2)
    return (0, 1)


def kept_open(s):
    return (NB - 2, NB - 1) if s == 0 else ()


def late_blocks(s):
    return tuple(d for d in range(NB) if d not in early_blocks(s))


F32 = mybir.dt.float32
BF16 = mybir.dt.bfloat16
U16 = mybir.dt.uint16
ADD = mybir.AluOpType.add
FUNC = mybir.ActivationFunctionType
SCALE = 1.0 / math.sqrt(D)

FLOPS = 3 * 2 * D * D * B * T + 2 * 2 * B * T * T * D


def block(i):
    return slice(i * P, (i + 1) * P)


def tile_attentionwithpositionalencoding_b_kernel(tc, table, pe, wq, bq, wk, wv, bv, offs, out):
    nc = tc.nc
    with ExitStack() as ctx:
        held = ctx.enter_context(tc.tile_pool(name="held", bufs=1))
        pair = ctx.enter_context(tc.tile_pool(name="pair", bufs=2))
        ring = ctx.enter_context(tc.tile_pool(name="ring", bufs=4))
        many = ctx.enter_context(tc.tile_pool(name="many", bufs=8))
        psum = ctx.enter_context(tc.psum_pool(name="psum", bufs=8))

        offsets = held.tile([P, B * T // 16], U16, name="offsets")
        nc.sync.dma_start(offsets[:], offs)
        table_sb = [held.tile([P, V], F32, name=f"table{d}") for d in range(NB)]
        pe_sb = [held.tile([P, T], F32, name=f"pe{d}") for d in range(NB)]
        wq_sb = [held.tile([P, D], BF16, name=f"wq{d}") for d in range(NB)]
        wk_sb = [held.tile([P, D], BF16, name=f"wk{d}") for d in range(NB)]
        wv_sb = [held.tile([P, D], BF16, name=f"wv{d}") for d in range(NB)]
        for d in range(NB):
            nc.sync.dma_start(pe_sb[d][:], pe[block(d), :])
            nc.sync.dma_start(table_sb[d][:], table[block(d), :])
            nc.sync.dma_start(wq_sb[d][:], wq[block(d), :])
            nc.sync.dma_start(wk_sb[d][:], wk[block(d), :])
        bq_sb = held.tile([P, NB], F32, name="bq_sb")
        with nc.allow_non_contiguous_dma(reason="512 biases, one to a partition"):
            nc.sync.dma_start(bq_sb[:], bq.rearrange("(m p) o -> p (m o)", p=P))
        for d in range(NB):
            nc.sync.dma_start(wv_sb[d][:], wv[block(d), :])
        bv_all = held.tile([P, D], F32, name="bv_all")
        nc.sync.dma_start(bv_all[:], bv.rearrange("d o -> (d o)").partition_broadcast(P))
        ident = held.tile([P, P], BF16, name="ident")
        make_identity(nc, ident[:])

        e_bf = [[held.tile([P, T], BF16, name=f"e{d}_{s}") for s in range(B)] for d in range(NB)]

        strip = held.tile([P, 2 * T], F32, name="strip")
        LEFT, RIGHT, ACROSS = 0, T, T // 2

        def embed(d, s, start):
            e32 = strip[:, start : start + T]
            picked = table_sb[d][:].indirect(offsets[:, s * (T // 16) : (s + 1) * (T // 16)])
            nc.vector.tensor_tensor(e32, picked, pe_sb[d][:], ADD)
            nc.vector.tensor_copy(e_bf[d][s][:], e32)

        def nothing(*unused):
            pass

        def transposer(a_bf, at_bf):
            todo = [(i, j) for i in range(NB) for j in range(NB)]
            banks = []

            def carry():
                if todo:
                    i, j = todo[0]
                    todo.remove((i, j))
                    if j == 0:
                        banks.append(psum.tile([P, NB, P], BF16, name="flipped", tag="bank"))
                    nc.tensor.transpose(banks[i][:, j, :], a_bf[i][:, block(j)], ident[:])
                    if j == NB - 1:
                        nc.scalar.copy(at_bf[:, :, block(i)], banks[i][:])

            return carry

        def add_qk(s, m, d, last, sums, carry):
            first = m not in sums
            if first:
                q_acc = psum.tile([P, T], F32, name="q_acc", tag="bank")
                k_acc = psum.tile([P, T], F32, name="k_acc", tag="bank")
                sums[m] = (q_acc, k_acc)
            q_acc, k_acc = sums[m]
            nc.tensor.matmul(q_acc[:], wq_sb[d][:, block(m)], e_bf[d][s][:], start=first, stop=last)
            carry()
            nc.tensor.matmul(k_acc[:], wk_sb[d][:, block(m)], e_bf[d][s][:], start=first, stop=last)
            carry()

        def project_qk_early(s, block_by_block):
            q_part = {m: held.tile([P, T], F32, name=f"q_part{s}_{m}") for m in range(NB) if m not in kept_open(s)}
            k_part = {m: held.tile([P, T], F32, name=f"k_part{s}_{m}") for m in range(NB) if m not in kept_open(s)}
            blocks = early_blocks(s)
            if block_by_block:
                order = [(d, m) for d in blocks for m in range(NB)]
            else:
                order = [(d, m) for m in range(NB) for d in blocks]
            sums = {}
            for d, m in order:
                parks = d == blocks[-1] and m not in kept_open(s)
                add_qk(s, m, d, parks, sums, nothing)
                if parks:
                    q_acc, k_acc = sums.pop(m)
                    nc.scalar.copy(q_part[m][:], q_acc[:])
                    nc.scalar.copy(k_part[m][:], k_acc[:])
            return q_part, k_part, sums

        def project_qk_late(s, parts, carry, after_block):
            q_part, k_part, sums = parts
            q_bf = [pair.tile([P, T], BF16, name=f"q{m}") for m in range(NB)]
            k_bf = [pair.tile([P, T], BF16, name=f"k{m}") for m in range(NB)]
            blocks = late_blocks(s)
            for m in range(NB):
                for d in blocks:
                    add_qk(s, m, d, d == blocks[-1], sums, carry)
                q_acc, k_acc = sums[m]
                if m in kept_open(s):
                    nc.scalar.activation(q_bf[m][:], q_acc[:], FUNC.Identity, bias=bq_sb[:, m : m + 1])
                    nc.scalar.copy(k_bf[m][:], k_acc[:])
                else:
                    nc.vector.scalar_tensor_tensor(q_bf[m][:], q_acc[:], bq_sb[:, m : m + 1], q_part[m][:], ADD, ADD)
                    nc.vector.tensor_tensor(k_bf[m][:], k_acc[:], k_part[m][:], ADD)
                after_block(m)
            return q_bf, k_bf

        def project_v(s, j, vt_bf, carry):
            acc = psum.tile([P, D], F32, name="acc", tag="bank")
            for d in range(NB):
                nc.tensor.matmul(acc[:], e_bf[d][s][:, block(j)], wv_sb[d][:], start=(d == 0), stop=(d == NB - 1))
                carry()
            nc.vector.tensor_tensor(vt_bf[j][:], acc[:], bv_all[:], ADD)

        def attention_weights(q_bf, k_bf):
            grown, total, a_bf = [], [], []
            for i in range(NB + 1):
                if i < NB:
                    score = psum.tile([P, T], F32, name="score", tag="bank")
                    for m in range(NB):
                        nc.tensor.matmul(score[:], q_bf[m][:, block(i)], k_bf[m][:], start=(m == 0), stop=(m == NB - 1))
                    top = many.tile([P, 1], F32, name="top")
                    nc.vector.reduce_max(top[:], score[:], axis=mybir.AxisListType.X)
                    shift = many.tile([P, 1], F32, name="shift")
                    nc.vector.tensor_scalar_mul(shift[:], top[:], -SCALE)
                    grown.append(ring.tile([P, T], F32, name="grown"))
                    total.append(many.tile([P, 1], F32, name="total"))
                    nc.scalar.activation(
                        grown[i][:], score[:], FUNC.Exp, bias=shift[:], scale=SCALE, accum_out=total[i][:]
                    )
                if i > 0:
                    share = many.tile([P, 1], F32, name="share")
                    nc.vector.reciprocal(share[:], total[i - 1][:])
                    a_bf.append(many.tile([P, T], BF16, name="a_i"))
                    nc.vector.tensor_scalar_mul(a_bf[i - 1][:], grown[i - 1][:], share[:])
            return a_bf

        def attend(s, vt_bf, at_bf, feature_blocks, carry, ends=(T,)):
            for m in feature_blocks:
                out_sb = ring.tile([P, T], F32, name="out_sb")
                begin = 0
                for end in ends:
                    queries, width = slice(begin, end), end - begin
                    mixed = psum.tile([P, T], F32, name="mixed", tag="bank")
                    for j in range(NB):
                        nc.tensor.matmul(
                            mixed[:, :width], vt_bf[j][:, block(m)], at_bf[:, j, queries], start=(j == 0), stop=(j == NB - 1)
                        )
                        carry()
                    nc.scalar.copy(out_sb[:, queries], mixed[:, :width])
                    nc.sync.dma_start(out[block(m), s * T + begin : s * T + end], out_sb[:, queries])
                    begin = end

        last_first = [B - 1] + list(range(B - 1))
        embed(0, B - 1, ACROSS)
        embed(0, 0, LEFT)
        embed(0, 1, RIGHT)
        embed(1, 0, ACROSS)
        by_need = [(1, 1), (0, B - 2), (1, B - 2), (2, B - 2), (2, 0), (3, 0)]
        turns = []

        def embed_in_turn(blocks):
            for d, s in blocks:
                embed(d, s, LEFT if len(turns) % 2 == 0 else RIGHT)
                turns.append((d, s))

        embed_in_turn(by_need + [(d, 1) for d in late_blocks(1)])
        parked = {}
        for s in last_first[:-1]:
            parked[s] = project_qk_early(s, block_by_block=(s == 0))
        parked[B - 2] = project_qk_early(B - 2, block_by_block=False)
        q_bf, k_bf = project_qk_late(0, parked[0], nothing, nothing)

        first_half, second_half = range(NB // 2), range(NB // 2, NB)
        before = None
        for s in range(B):
            a_bf = attention_weights(q_bf, k_bf)
            vt_bf = [pair.tile([P, D], BF16, name=f"vt{j}") for j in range(NB)]
            at_bf = pair.tile([P, NB, T], BF16, name="at_bf")
            carry = transposer(a_bf, at_bf)
            for j in range(NB):
                project_v(s, j, vt_bf, nothing if s == 0 and j < NB // 2 else carry)

            def kept_back(m):
                if before is not None and m < len(second_half):
                    attend(s - 1, before[0], before[1], second_half[m : m + 1], carry)

            if s + 1 < B:
                q_bf, k_bf = project_qk_late(s + 1, parked[s + 1], carry, kept_back)
            else:
                for m in range(NB):
                    kept_back(m)
            attend(s, vt_bf, at_bf, first_half, nothing)
            before = (vt_bf, at_bf)
            if s + 2 < B:
                embed_in_turn([(d, s + 2) for d in late_blocks(s + 2)])
        attend(B - 1, vt_bf, at_bf, second_half[:1], nothing)
        attend(B - 1, vt_bf, at_bf, second_half[1:], nothing, ends=(3 * T // 4, T))
